import numpy as np
import ml_dtypes


def mxq(x, axis, fmt="e4m3"):
    dtype, down = {"e4m3": (ml_dtypes.float8_e4m3fn, 7), "e5m2": (ml_dtypes.float8_e5m2, 14)}[fmt]
    v = np.moveaxis(np.asarray(x, np.float32).astype(ml_dtypes.bfloat16).astype(np.float64), axis, -1)
    blocks = v.reshape(v.shape[:-1] + (-1, 32))
    amax = np.abs(blocks).max(-1, keepdims=True)
    byte = np.maximum(np.where(amax > 0, np.frexp(amax)[1] - 1 + 127, 0) - down, 1)
    scale = np.exp2(byte - 127.0)
    codes = (blocks / scale).astype(np.float32).astype(dtype).astype(np.float64)
    return np.moveaxis((codes * scale).reshape(v.shape), -1, axis)


WIDE = False


def mx_kscale(k):
    if not WIDE:
        return np.ones(k)
    levels = np.array([10, -10, 5, -5, 0])
    a = np.random.permutation(np.resize(levels, k // 512 * 4)).reshape(k // 512, 4)
    idx = np.arange(k)
    return np.exp2(a[idx // 512, idx % 128 // 32])


BF16 = ml_dtypes.bfloat16


def bf(x):
    return np.asarray(x, np.float32).astype(BF16)


def f64(x):
    return np.asarray(x).astype(np.float64)


B, N, D, H, W = 2, 4096, 512, 8, 256
HD = D // H
DF = N * HD // W


def setup_inputs():
    s = mx_kscale(D)
    u = mx_kscale(D)
    r = np.concatenate([u, 1.0 / u])
    return {"x": bf(np.random.standard_normal((B, N, D)) * s),
            "Wqk": bf(np.random.standard_normal((2 * D, D)) * 0.8 / np.sqrt(D) * r[:, None] / s)}


def reference(x, Wqk):
    qk = mxq(f64(x), 2, "e4m3") @ mxq(f64(Wqk), 1, "e4m3").T
    qk = qk.reshape(B, N, 2, H, HD).transpose(2, 0, 3, 1, 4)
    q = (qk[0] * HD ** -0.5).reshape(B * H, W, DF)
    k = qk[1].reshape(B * H, W, DF)
    s = mxq(q, 2, "e4m3") @ mxq(k, 2, "e4m3").transpose(0, 2, 1)
    e = np.exp(s - s.max(-1, keepdims=True))
    return e / e.sum(-1, keepdims=True)

@@ -1,0 +1,227 @@
+from contextlib import ExitStack
+
+import concourse.mybir as mybir
+from concourse.masks import make_identity
+
+F32 = mybir.dt.float32
+BF16 = mybir.dt.bfloat16
+I32 = mybir.dt.int32
+U32 = mybir.dt.uint32
+U8 = mybir.dt.uint8
+FP8X4 = mybir.dt.float8_e4m3fn_x4
+ACT = mybir.ActivationFunctionType
+
+P = 128
+PACK = 4
+BATCH, TOKENS, MODEL = 2, 4096, 512
+HEADS, HEAD_DIM, ROWS = 8, 64, 256
+PER_ROW = TOKENS // ROWS
+PAIRS = HEADS // 2
+J_GROUPS = PER_ROW // PACK
+ROW_HALVES = ROWS // P
+CHUNKS = J_GROUPS * ROW_HALVES
+CHUNK = P * PACK
+WORDS = MODEL // 2
+QUERY_FACTOR = HEAD_DIM ** -0.5
+UNITS = BATCH * PAIRS
+GROUP = 4
+VECTOR_EVERY = 4
+
+FLOPS = 2 * BATCH * TOKENS * MODEL * 2 * MODEL + 2 * BATCH * HEADS * ROWS * ROWS * PER_ROW * HEAD_DIM
+
+
+def tile_slidingwindowattention_pa_t_kernel(tc, x, Wqk, out):
+    nc = tc.nc
+    with ExitStack() as ctx:
+        keep = ctx.enter_context(tc.tile_pool(name="keep", bufs=1))
+        x_pool = ctx.enter_context(tc.tile_pool(name="x_pool", bufs=BATCH * CHUNKS))
+        w_pool = ctx.enter_context(tc.tile_pool(name="w_pool", bufs=PAIRS))
+        stage = ctx.enter_context(tc.tile_pool(name="stage", bufs=3))
+        g_pool = ctx.enter_context(tc.tile_pool(name="g_pool", bufs=4))
+        qk_pool = ctx.enter_context(tc.tile_pool(name="qk_pool", bufs=2))
+        soft = ctx.enter_context(tc.tile_pool(name="soft", bufs=4))
+        turn_psum = ctx.enter_context(tc.psum_pool(name="turn_psum", bufs=2))
+        proj_psum = ctx.enter_context(tc.psum_pool(name="proj_psum", bufs=4))
+        score_psum = ctx.enter_context(tc.psum_pool(name="score_psum", bufs=2))
+
+        w_view = Wqk.rearrange("(s hp p) d -> hp p s d", s=2, hp=PAIRS, p=P)
+        x_view = x.rearrange(
+            "b (rh w jg jj) d -> b jg rh w (jj d)", rh=ROW_HALVES, w=P, jg=J_GROUPS, jj=PACK
+        )
+        w_raw = []
+        x_raw = []
+
+        def load_w(hp):
+            w_tile = w_pool.tile([P, 2 * MODEL], BF16)
+            nc.sync.dma_start(out=w_tile[:].rearrange("p (s d) -> p s d", s=2), in_=w_view[hp])
+            w_raw.append(w_tile)
+
+        def load_x(b, c):
+            x_tile = x_pool.tile([P, PACK * MODEL], BF16)
+            nc.sync.dma_start(out=x_tile[:], in_=x_view[b, c // ROW_HALVES, c % ROW_HALVES])
+            x_raw.append(x_tile)
+
+        load_w(0)
+        load_x(0, 0)
+        load_x(0, 1)
+        for hp in range(1, PAIRS):
+            load_w(hp)
+        for c in range(2, CHUNKS):
+            load_x(0, c)
+        for c in range(CHUNKS):
+            load_x(1, c)
+
+        ident = keep.tile([P, P], F32)
+        make_identity(nc, ident[:])
+        warm_in = keep.tile([P, 1], F32)
+        warm_out = keep.tile([P, 1], F32)
+        nc.vector.memset(warm_in[:], 0.0)
+        nc.scalar.activation(out=warm_out[:], in_=warm_in[:], func=ACT.Exp)
+
+        w_codes = keep.tile([P, PAIRS * 2 * P], U32, align_bytes=64)
+        w_scales = keep.tile([P, PAIRS * 2 * P], U8, align_bytes=64)
+        x_codes = keep.tile([P, BATCH * CHUNKS * CHUNK], U32, align_bytes=64)
+        x_scales = keep.tile([P, BATCH * CHUNKS * CHUNK], U8, align_bytes=64)
+        k_split = []
+        for parity in range(2):
+            k_split_tile = keep.tile([P, 2, J_GROUPS * ROWS], U32, name="k_split%d" % parity, align_bytes=64)
+            nc.vector.memset(k_split_tile[:].bitcast(I32), 0)
+            k_split.append(k_split_tile)
+
+        def leave_psum(on_vector, dst, src, factor):
+            if on_vector:
+                nc.vector.tensor_scalar_mul(out=dst, in0=src, scalar1=factor)
+            else:
+                nc.scalar.activation(out=dst, in_=src, func=ACT.Copy, scale=factor)
+
+        def turn(raw, pieces, grouped):
+            raw_words = raw[:].bitcast(F32)
+            grouped_words = grouped[:].bitcast(F32).rearrange("p (n r u) -> p n r u", r=P, u=2)
+            for bank in range(pieces // 2):
+                turned = turn_psum.tile([P, 2 * 2 * P], F32)
+                for n in range(2):
+                    for u in range(2):
+                        first = (2 * bank + n) * WORDS + u * P
+                        nc.tensor.transpose(
+                            turned[:, (2 * n + u) * P : (2 * n + u + 1) * P],
+                            raw_words[:, first : first + P],
+                            ident[:],
+                        )
+                dst = grouped_words[:, 2 * bank : 2 * bank + 2, :, :]
+                src = turned[:].rearrange("p (n u r) -> p n r u", n=2, u=2)
+                if bank % 2 == 1:
+                    nc.vector.tensor_copy(out=dst, in_=src)
+                else:
+                    nc.scalar.copy(out=dst, in_=src)
+
+        def prepare_w(hp):
+            w_grouped = stage.tile([P, 2 * P * PACK], BF16, align_bytes=64)
+            turn(w_raw[hp], 2, w_grouped)
+            cols = slice(hp * 2 * P, (hp + 1) * 2 * P)
+            nc.vector.quantize_mx(
+                out=w_codes[:, cols].bitcast(FP8X4), scales=w_scales[:, cols], in_=w_grouped[:]
+            )
+
+        def prepare_x(b, c):
+            x_grouped = stage.tile([P, CHUNK * PACK], BF16, align_bytes=64)
+            turn(x_raw[b * CHUNKS + c], PACK, x_grouped)
+            cols = slice((b * CHUNKS + c) * CHUNK, (b * CHUNKS + c + 1) * CHUNK)
+            nc.vector.quantize_mx(
+                out=x_codes[:, cols].bitcast(FP8X4), scales=x_scales[:, cols], in_=x_grouped[:]
+            )
+
+        def project(unit):
+            b, hp = divmod(unit, PAIRS)
+            q_codes = qk_pool.tile([P, J_GROUPS * ROWS], U32, align_bytes=64)
+            q_scales = qk_pool.tile([P, J_GROUPS * ROWS], U8, align_bytes=64)
+            k_codes = qk_pool.tile([P, J_GROUPS * ROWS], U32, align_bytes=64)
+            k_scales = qk_pool.tile([P, J_GROUPS * ROWS], U8, align_bytes=64)
+            codes = [q_codes, k_codes]
+            scales = [q_scales, k_scales]
+            for first_chunk in range(0, CHUNKS, GROUP):
+                for s in range(2):
+                    w_cols = slice((hp * 2 + s) * P, (hp * 2 + s + 1) * P)
+                    grouped = g_pool.tile([P, GROUP * CHUNK], BF16, align_bytes=64)
+                    for i in range(GROUP):
+                        c = b * CHUNKS + first_chunk + i
+                        x_cols = slice(c * CHUNK, (c + 1) * CHUNK)
+                        acc = proj_psum.tile([P, CHUNK], F32)
+                        nc.tensor.matmul_mx(
+                            out=acc[:],
+                            lhsT=w_codes[:, w_cols].bitcast(FP8X4),
+                            lhsT_scale=w_scales[:, w_cols],
+                            rhs=x_codes[:, x_cols].bitcast(FP8X4),
+                            rhs_scale=x_scales[:, x_cols],
+                            start=True,
+                            stop=True,
+                        )
+                        leave_psum(
+                            i % VECTOR_EVERY == VECTOR_EVERY - 1,
+                            grouped[:, i * CHUNK : (i + 1) * CHUNK].rearrange("p (w j) -> p w j", j=PACK),
+                            acc[:].rearrange("p (j w) -> p w j", j=PACK),
+                            QUERY_FACTOR if s == 0 else 1.0,
+                        )
+                    cols = slice(first_chunk * P, (first_chunk + GROUP) * P)
+                    nc.vector.quantize_mx(
+                        out=codes[s][:, cols].bitcast(FP8X4), scales=scales[s][:, cols], in_=grouped[:]
+                    )
+            split = k_split[unit % 2]
+            half = P // 2
+            nc.sync.dma_start(out=split[0:half, 0, :].bitcast(I32), in_=k_codes[0:half, :].bitcast(I32))
+            nc.sync.dma_start(out=split[half:P, 1, :].bitcast(I32), in_=k_codes[half:P, :].bitcast(I32))
+            return q_codes, q_scales, split, k_scales
+
+        def attend(unit, q_codes, q_scales, split, k_scales):
+            for h in range(2):
+                score = score_psum.tile([P, ROW_HALVES, ROWS], F32)
+                for rh in range(ROW_HALVES):
+                    for jg in range(J_GROUPS):
+                        q_cols = slice(jg * ROWS + rh * P, jg * ROWS + (rh + 1) * P)
+                        k_cols = slice(jg * ROWS, (jg + 1) * ROWS)
+                        nc.tensor.matmul_mx(
+                            out=score[:, rh, :],
+                            lhsT=q_codes[:, q_cols].bitcast(FP8X4),
+                            lhsT_scale=q_scales[:, q_cols],
+                            rhs=split[:, h, k_cols].bitcast(FP8X4),
+                            rhs_scale=k_scales[:, k_cols],
+                            start=(jg == 0),
+                            stop=(jg == J_GROUPS - 1),
+                        )
+                minus_max = soft.tile([P, ROW_HALVES], F32)
+                nc.vector.tensor_reduce(
+                    out=minus_max[:], in_=score[:], axis=mybir.AxisListType.X, op=mybir.AluOpType.max, negate=True
+                )
+                weights = soft.tile([P, ROW_HALVES, ROWS], F32)
+                row_sum = soft.tile([P, ROW_HALVES], F32)
+                for rh in range(ROW_HALVES):
+                    nc.scalar.activation(
+                        out=weights[:, rh, :],
+                        in_=score[:, rh, :],
+                        func=ACT.Exp,
+                        bias=minus_max[:, rh : rh + 1],
+                        accum_out=row_sum[:, rh : rh + 1],
+                    )
+                inverse = soft.tile([P, ROW_HALVES], F32)
+                nc.vector.reciprocal(out=inverse[:], in_=row_sum[:])
+                for rh in range(ROW_HALVES):
+                    nc.vector.tensor_scalar_mul(
+                        out=weights[:, rh, :], in0=weights[:, rh, :], scalar1=inverse[:, rh : rh + 1]
+                    )
+                nc.sync.dma_start(
+                    out=out[unit * 2 + h].rearrange("(rh w) c -> w rh c", rh=ROW_HALVES), in_=weights[:]
+                )
+
+        prepare_w(0)
+        for c in range(CHUNKS):
+            prepare_x(0, c)
+        for hp in range(1, PAIRS):
+            prepare_w(hp)
+        ready = project(0)
+        for unit in range(UNITS):
+            if unit < PAIRS:
+                prepare_x(1, 2 * unit)
+                prepare_x(1, 2 * unit + 1)
+            current = ready
+            if unit + 1 < UNITS:
+                ready = project(unit + 1)
+            attend(unit, *current)

@@ -25,7 +25,13 @@ WORDS = MODEL // 2
 QUERY_FACTOR = HEAD_DIM ** -0.5
 UNITS = BATCH * PAIRS
 GROUP = 4
-VECTOR_EVERY = 4
+UNIT_GROUPS = 4
+GROUPS = UNITS * UNIT_GROUPS
+UNIT_WORDS = J_GROUPS * ROWS
+VECTOR_EVERY = 3
+TURN_AHEAD = 2
+SCORE_LAG = 4
+DRAIN = SCORE_LAG + 2
 
 FLOPS = 2 * BATCH * TOKENS * MODEL * 2 * MODEL + 2 * BATCH * HEADS * ROWS * ROWS * PER_ROW * HEAD_DIM
 
@@ -40,36 +46,32 @@ def tile_slidingwindowattention_pa_t_kernel(tc, x, Wqk, out):
         g_pool = ctx.enter_context(tc.tile_pool(name="g_pool", bufs=4))
         qk_pool = ctx.enter_context(tc.tile_pool(name="qk_pool", bufs=2))
         soft = ctx.enter_context(tc.tile_pool(name="soft", bufs=4))
-        turn_psum = ctx.enter_context(tc.psum_pool(name="turn_psum", bufs=2))
-        proj_psum = ctx.enter_context(tc.psum_pool(name="proj_psum", bufs=4))
+        bank_psum = ctx.enter_context(tc.psum_pool(name="bank_psum", bufs=6))
         score_psum = ctx.enter_context(tc.psum_pool(name="score_psum", bufs=2))
+        ctx.enter_context(tc.manual_schedule())
 
         w_view = Wqk.rearrange("(s hp p) d -> hp p s d", s=2, hp=PAIRS, p=P)
         x_view = x.rearrange(
             "b (rh w jg jj) d -> b jg rh w (jj d)", rh=ROW_HALVES, w=P, jg=J_GROUPS, jj=PACK
         )
-        w_raw = []
-        x_raw = []
+        w_raw = {}
+        x_raw = {}
 
         def load_w(hp):
             w_tile = w_pool.tile([P, 2 * MODEL], BF16)
             nc.sync.dma_start(out=w_tile[:].rearrange("p (s d) -> p s d", s=2), in_=w_view[hp])
-            w_raw.append(w_tile)
+            w_raw[hp] = w_tile
 
         def load_x(b, c):
             x_tile = x_pool.tile([P, PACK * MODEL], BF16)
             nc.sync.dma_start(out=x_tile[:], in_=x_view[b, c // ROW_HALVES, c % ROW_HALVES])
-            x_raw.append(x_tile)
+            x_raw[(b, c)] = x_tile
 
         load_w(0)
-        load_x(0, 0)
-        load_x(0, 1)
+        for c in range(CHUNKS):
+            load_x(0, c)
         for hp in range(1, PAIRS):
             load_w(hp)
-        for c in range(2, CHUNKS):
-            load_x(0, c)
-        for c in range(CHUNKS):
-            load_x(1, c)
 
         ident = keep.tile([P, P], F32)
         make_identity(nc, ident[:])
@@ -84,21 +86,18 @@ def tile_slidingwindowattention_pa_t_kernel(tc, x, Wqk, out):
         x_scales = keep.tile([P, BATCH * CHUNKS * CHUNK], U8, align_bytes=64)
         k_split = []
         for parity in range(2):
-            k_split_tile = keep.tile([P, 2, J_GROUPS * ROWS], U32, name="k_split%d" % parity, align_bytes=64)
+            k_split_tile = keep.tile([P, 2, UNIT_WORDS], U32, name="k_split%d" % parity, align_bytes=64)
             nc.vector.memset(k_split_tile[:].bitcast(I32), 0)
             k_split.append(k_split_tile)
 
-        def leave_psum(on_vector, dst, src, factor):
-            if on_vector:
-                nc.vector.tensor_scalar_mul(out=dst, in0=src, scalar1=factor)
-            else:
-                nc.scalar.activation(out=dst, in_=src, func=ACT.Copy, scale=factor)
+        def on_vector(bank_number):
+            return bank_number % VECTOR_EVERY == VECTOR_EVERY - 1
 
-        def turn(raw, pieces, grouped):
+        def turn(raw, pieces, grouped, first_bank):
             raw_words = raw[:].bitcast(F32)
             grouped_words = grouped[:].bitcast(F32).rearrange("p (n r u) -> p n r u", r=P, u=2)
             for bank in range(pieces // 2):
-                turned = turn_psum.tile([P, 2 * 2 * P], F32)
+                turned = bank_psum.tile([P, 2 * 2 * P], F32, tag="bank")
                 for n in range(2):
                     for u in range(2):
                         first = (2 * bank + n) * WORDS + u * P
@@ -109,119 +108,178 @@ def tile_slidingwindowattention_pa_t_kernel(tc, x, Wqk, out):
                         )
                 dst = grouped_words[:, 2 * bank : 2 * bank + 2, :, :]
                 src = turned[:].rearrange("p (n u r) -> p n r u", n=2, u=2)
-                if bank % 2 == 1:
+                if on_vector(first_bank + bank):
                     nc.vector.tensor_copy(out=dst, in_=src)
                 else:
                     nc.scalar.copy(out=dst, in_=src)
 
         def prepare_w(hp):
             w_grouped = stage.tile([P, 2 * P * PACK], BF16, align_bytes=64)
-            turn(w_raw[hp], 2, w_grouped)
+            turn(w_raw[hp], 2, w_grouped, hp)
             cols = slice(hp * 2 * P, (hp + 1) * 2 * P)
             nc.vector.quantize_mx(
                 out=w_codes[:, cols].bitcast(FP8X4), scales=w_scales[:, cols], in_=w_grouped[:]
             )
 
-        def prepare_x(b, c):
+        def turn_x(b, c):
             x_grouped = stage.tile([P, CHUNK * PACK], BF16, align_bytes=64)
-            turn(x_raw[b * CHUNKS + c], PACK, x_grouped)
+            turn(x_raw[(b, c)], PACK, x_grouped, (b * CHUNKS + c) * 2)
+            return b, c, x_grouped
+
+        def quantise_x(b, c, x_grouped):
             cols = slice((b * CHUNKS + c) * CHUNK, (b * CHUNKS + c + 1) * CHUNK)
             nc.vector.quantize_mx(
                 out=x_codes[:, cols].bitcast(FP8X4), scales=x_scales[:, cols], in_=x_grouped[:]
             )
 
-        def project(unit):
-            b, hp = divmod(unit, PAIRS)
-            q_codes = qk_pool.tile([P, J_GROUPS * ROWS], U32, align_bytes=64)
-            q_scales = qk_pool.tile([P, J_GROUPS * ROWS], U8, align_bytes=64)
-            k_codes = qk_pool.tile([P, J_GROUPS * ROWS], U32, align_bytes=64)
-            k_scales = qk_pool.tile([P, J_GROUPS * ROWS], U8, align_bytes=64)
-            codes = [q_codes, k_codes]
-            scales = [q_scales, k_scales]
-            for first_chunk in range(0, CHUNKS, GROUP):
-                for s in range(2):
-                    w_cols = slice((hp * 2 + s) * P, (hp * 2 + s + 1) * P)
-                    grouped = g_pool.tile([P, GROUP * CHUNK], BF16, align_bytes=64)
-                    for i in range(GROUP):
-                        c = b * CHUNKS + first_chunk + i
-                        x_cols = slice(c * CHUNK, (c + 1) * CHUNK)
-                        acc = proj_psum.tile([P, CHUNK], F32)
-                        nc.tensor.matmul_mx(
-                            out=acc[:],
-                            lhsT=w_codes[:, w_cols].bitcast(FP8X4),
-                            lhsT_scale=w_scales[:, w_cols],
-                            rhs=x_codes[:, x_cols].bitcast(FP8X4),
-                            rhs_scale=x_scales[:, x_cols],
-                            start=True,
-                            stop=True,
-                        )
-                        leave_psum(
-                            i % VECTOR_EVERY == VECTOR_EVERY - 1,
-                            grouped[:, i * CHUNK : (i + 1) * CHUNK].rearrange("p (w j) -> p w j", j=PACK),
-                            acc[:].rearrange("p (j w) -> p w j", j=PACK),
-                            QUERY_FACTOR if s == 0 else 1.0,
-                        )
-                    cols = slice(first_chunk * P, (first_chunk + GROUP) * P)
-                    nc.vector.quantize_mx(
-                        out=codes[s][:, cols].bitcast(FP8X4), scales=scales[s][:, cols], in_=grouped[:]
-                    )
-            split = k_split[unit % 2]
-            half = P // 2
-            nc.sync.dma_start(out=split[0:half, 0, :].bitcast(I32), in_=k_codes[0:half, :].bitcast(I32))
-            nc.sync.dma_start(out=split[half:P, 1, :].bitcast(I32), in_=k_codes[half:P, :].bitcast(I32))
-            return q_codes, q_scales, split, k_scales
+        grouped_of = {}
+        codes_of = {}
+        score_of = {}
+        minus_max_of = {}
+        weights_of = {}
+        row_sum_of = {}
 
-        def attend(unit, q_codes, q_scales, split, k_scales):
+        def is_queries(g):
+            return 0 <= g < GROUPS and g % UNIT_GROUPS >= 2
+
+        def project(g, i):
+            unit, part = divmod(g, UNIT_GROUPS)
+            b, hp = divmod(unit, PAIRS)
+            queries, half = divmod(part, 2)
+            if i == 0:
+                grouped_of[g] = g_pool.tile([P, GROUP * CHUNK], BF16, name="grouped", align_bytes=64)
+            c = i * ROW_HALVES + half if queries else half * GROUP + i
+            w_cols = slice((hp * 2 + 1 - queries) * P, (hp * 2 + 2 - queries) * P)
+            x_cols = slice((b * CHUNKS + c) * CHUNK, (b * CHUNKS + c + 1) * CHUNK)
+            acc = bank_psum.tile([P, CHUNK], F32, tag="bank")
+            nc.tensor.matmul_mx(
+                out=acc[:],
+                lhsT=w_codes[:, w_cols].bitcast(FP8X4),
+                lhsT_scale=w_scales[:, w_cols],
+                rhs=x_codes[:, x_cols].bitcast(FP8X4),
+                rhs_scale=x_scales[:, x_cols],
+                start=True,
+                stop=True,
+            )
+            dst = grouped_of[g][:, i * CHUNK : (i + 1) * CHUNK].rearrange("p (w j) -> p w j", j=PACK)
+            src = acc[:].rearrange("p (j w) -> p w j", j=PACK)
+            factor = QUERY_FACTOR if queries else 1.0
+            if on_vector(g * GROUP + i):
+                nc.vector.tensor_scalar_mul(out=dst, in0=src, scalar1=factor)
+            else:
+                nc.scalar.activation(out=dst, in_=src, func=ACT.Copy, scale=factor)
+
+        def quantise(g):
+            if not 0 <= g < GROUPS:
+                return
+            unit, part = divmod(g, UNIT_GROUPS)
+            queries, half = divmod(part, 2)
+            if half == 0:
+                codes = qk_pool.tile([P, UNIT_WORDS], U32, name="codes%d" % queries, align_bytes=64)
+                scales = qk_pool.tile([P, UNIT_WORDS], U8, name="scales%d" % queries, align_bytes=64)
+                codes_of[(unit, queries)] = (codes, scales)
+            codes, scales = codes_of[(unit, queries)]
+            cols = slice(half * GROUP * P, (half + 1) * GROUP * P)
+            nc.vector.quantize_mx(
+                out=codes[:, cols].bitcast(FP8X4), scales=scales[:, cols], in_=grouped_of[g][:]
+            )
+            if part == 1:
+                split = k_split[unit % 2]
+                nc.sync.dma_start(out=split[0 : P // 2, 0, :].bitcast(I32), in_=codes[0 : P // 2, :].bitcast(I32))
+                nc.sync.dma_start(out=split[P // 2 : P, 1, :].bitcast(I32), in_=codes[P // 2 : P, :].bitcast(I32))
+
+        def scores(g):
+            if not is_queries(g):
+                return
+            unit, rh = g // UNIT_GROUPS, g % 2
+            q_codes, q_scales = codes_of[(unit, 1)]
+            k_scales = codes_of[(unit, 0)][1]
+            split = k_split[unit % 2]
+            score = score_psum.tile([P, 2, ROWS], F32)
             for h in range(2):
-                score = score_psum.tile([P, ROW_HALVES, ROWS], F32)
-                for rh in range(ROW_HALVES):
-                    for jg in range(J_GROUPS):
-                        q_cols = slice(jg * ROWS + rh * P, jg * ROWS + (rh + 1) * P)
-                        k_cols = slice(jg * ROWS, (jg + 1) * ROWS)
-                        nc.tensor.matmul_mx(
-                            out=score[:, rh, :],
-                            lhsT=q_codes[:, q_cols].bitcast(FP8X4),
-                            lhsT_scale=q_scales[:, q_cols],
-                            rhs=split[:, h, k_cols].bitcast(FP8X4),
-                            rhs_scale=k_scales[:, k_cols],
-                            start=(jg == 0),
-                            stop=(jg == J_GROUPS - 1),
-                        )
-                minus_max = soft.tile([P, ROW_HALVES], F32)
-                nc.vector.tensor_reduce(
-                    out=minus_max[:], in_=score[:], axis=mybir.AxisListType.X, op=mybir.AluOpType.max, negate=True
-                )
-                weights = soft.tile([P, ROW_HALVES, ROWS], F32)
-                row_sum = soft.tile([P, ROW_HALVES], F32)
-                for rh in range(ROW_HALVES):
-                    nc.scalar.activation(
-                        out=weights[:, rh, :],
-                        in_=score[:, rh, :],
-                        func=ACT.Exp,
-                        bias=minus_max[:, rh : rh + 1],
-                        accum_out=row_sum[:, rh : rh + 1],
+                for jg in range(J_GROUPS):
+                    q_cols = slice((rh * J_GROUPS + jg) * P, (rh * J_GROUPS + jg + 1) * P)
+                    k_cols = slice(jg * ROWS, (jg + 1) * ROWS)
+                    nc.tensor.matmul_mx(
+                        out=score[:, h, :],
+                        lhsT=q_codes[:, q_cols].bitcast(FP8X4),
+                        lhsT_scale=q_scales[:, q_cols],
+                        rhs=split[:, h, k_cols].bitcast(FP8X4),
+                        rhs_scale=k_scales[:, k_cols],
+                        start=(jg == 0),
+                        stop=(jg == J_GROUPS - 1),
                     )
-                inverse = soft.tile([P, ROW_HALVES], F32)
-                nc.vector.reciprocal(out=inverse[:], in_=row_sum[:])
-                for rh in range(ROW_HALVES):
-                    nc.vector.tensor_scalar_mul(
-                        out=weights[:, rh, :], in0=weights[:, rh, :], scalar1=inverse[:, rh : rh + 1]
-                    )
-                nc.sync.dma_start(
-                    out=out[unit * 2 + h].rearrange("(rh w) c -> w rh c", rh=ROW_HALVES), in_=weights[:]
+            score_of[g] = score
+
+        def row_max(g):
+            if not is_queries(g):
+                return
+            minus_max = soft.tile([P, 2], F32)
+            nc.vector.tensor_reduce(
+                out=minus_max[:], in_=score_of[g][:], axis=mybir.AxisListType.X, op=mybir.AluOpType.max, negate=True
+            )
+            minus_max_of[g] = minus_max
+
+        def exponentials(g):
+            if not is_queries(g):
+                return
+            weights = soft.tile([P, 2, ROWS], F32)
+            row_sum = soft.tile([P, 2], F32)
+            for h in range(2):
+                nc.scalar.activation(
+                    out=weights[:, h, :],
+                    in_=score_of[g][:, h, :],
+                    func=ACT.Exp,
+                    bias=minus_max_of[g][:, h : h + 1],
+                    accum_out=row_sum[:, h : h + 1],
                 )
+            weights_of[g] = weights
+            row_sum_of[g] = row_sum
+
+        def normalise_and_store(g):
+            if not is_queries(g):
+                return
+            unit, rh = g // UNIT_GROUPS, g % 2
+            weights = weights_of[g]
+            inverse = soft.tile([P, 2], F32)
+            nc.vector.reciprocal(out=inverse[:], in_=row_sum_of[g][:])
+            for h in range(2):
+                nc.vector.tensor_scalar_mul(
+                    out=weights[:, h, :], in0=weights[:, h, :], scalar1=inverse[:, h : h + 1]
+                )
+            nc.sync.dma_start(
+                out=out[unit * 2 : unit * 2 + 2, rh * P : (rh + 1) * P, :].rearrange("h w c -> w h c"),
+                in_=weights[:],
+            )
 
         prepare_w(0)
-        for c in range(CHUNKS):
-            prepare_x(0, c)
-        for hp in range(1, PAIRS):
-            prepare_w(hp)
-        ready = project(0)
-        for unit in range(UNITS):
-            if unit < PAIRS:
-                prepare_x(1, 2 * unit)
-                prepare_x(1, 2 * unit + 1)
-            current = ready
-            if unit + 1 < UNITS:
-                ready = project(unit + 1)
-            attend(unit, *current)
+        turned = None
+        for c in range(TURN_AHEAD):
+            if turned:
+                quantise_x(*turned)
+            turned = turn_x(0, c)
+        for g in range(GROUPS + DRAIN):
+            for i in range(GROUP):
+                step = g * GROUP + i
+                if i == 0 and g < CHUNKS:
+                    load_x(1, g)
+                before = turned
+                turned = None
+                if step + TURN_AHEAD < CHUNKS:
+                    turned = turn_x(0, step + TURN_AHEAD)
+                elif i == 0 and UNIT_GROUPS <= g < UNIT_GROUPS + CHUNKS:
+                    turned = turn_x(1, g - UNIT_GROUPS)
+                if before:
+                    quantise_x(*before)
+                if i == 2 and 1 <= g < PAIRS:
+                    prepare_w(g)
+                if g < GROUPS:
+                    project(g, i)
+                if i == 0:
+                    scores(g - SCORE_LAG)
+                    exponentials(g - SCORE_LAG - 1)
+                if i == 1:
+                    quantise(g - 1)
+                    row_max(g - SCORE_LAG)
+                if i == GROUP - 1:
+                    normalise_and_store(g - SCORE_LAG - 1)

@@ -29,8 +29,8 @@ UNIT_GROUPS = 4
 GROUPS = UNITS * UNIT_GROUPS
 UNIT_WORDS = J_GROUPS * ROWS
 VECTOR_EVERY = 3
-TURN_AHEAD = 2
-SCORE_LAG = 4
+TURN_AHEAD = 3
+SCORE_LAG = 3
 DRAIN = SCORE_LAG + 2
 
 FLOPS = 2 * BATCH * TOKENS * MODEL * 2 * MODEL + 2 * BATCH * HEADS * ROWS * ROWS * PER_ROW * HEAD_DIM
@@ -44,7 +44,8 @@ def tile_slidingwindowattention_pa_t_kernel(tc, x, Wqk, out):
         w_pool = ctx.enter_context(tc.tile_pool(name="w_pool", bufs=PAIRS))
         stage = ctx.enter_context(tc.tile_pool(name="stage", bufs=3))
         g_pool = ctx.enter_context(tc.tile_pool(name="g_pool", bufs=4))
-        qk_pool = ctx.enter_context(tc.tile_pool(name="qk_pool", bufs=2))
+        k_pool = ctx.enter_context(tc.tile_pool(name="k_pool", bufs=3))
+        q_pool = ctx.enter_context(tc.tile_pool(name="q_pool", bufs=2))
         soft = ctx.enter_context(tc.tile_pool(name="soft", bufs=4))
         bank_psum = ctx.enter_context(tc.psum_pool(name="bank_psum", bufs=6))
         score_psum = ctx.enter_context(tc.psum_pool(name="score_psum", bufs=2))
@@ -139,13 +140,19 @@ def tile_slidingwindowattention_pa_t_kernel(tc, x, Wqk, out):
         weights_of = {}
         row_sum_of = {}
 
+        order = []
+        for r in range(UNITS + 1):
+            if r < UNITS:
+                order.extend([(r, 0, 0), (r, 0, 1)])
+            if r >= 1:
+                order.extend([(r - 1, 1, 0), (r - 1, 1, 1)])
+
         def is_queries(g):
-            return 0 <= g < GROUPS and g % UNIT_GROUPS >= 2
+            return 0 <= g < GROUPS and order[g][1] == 1
 
         def project(g, i):
-            unit, part = divmod(g, UNIT_GROUPS)
+            unit, queries, half = order[g]
             b, hp = divmod(unit, PAIRS)
-            queries, half = divmod(part, 2)
             if i == 0:
                 grouped_of[g] = g_pool.tile([P, GROUP * CHUNK], BF16, name="grouped", align_bytes=64)
             c = i * ROW_HALVES + half if queries else half * GROUP + i
@@ -172,18 +179,18 @@ def tile_slidingwindowattention_pa_t_kernel(tc, x, Wqk, out):
         def quantise(g):
             if not 0 <= g < GROUPS:
                 return
-            unit, part = divmod(g, UNIT_GROUPS)
-            queries, half = divmod(part, 2)
+            unit, queries, half = order[g]
             if half == 0:
-                codes = qk_pool.tile([P, UNIT_WORDS], U32, name="codes%d" % queries, align_bytes=64)
-                scales = qk_pool.tile([P, UNIT_WORDS], U8, name="scales%d" % queries, align_bytes=64)
+                pool = q_pool if queries else k_pool
+                codes = pool.tile([P, UNIT_WORDS], U32, name="codes", align_bytes=64)
+                scales = pool.tile([P, UNIT_WORDS], U8, name="scales", align_bytes=64)
                 codes_of[(unit, queries)] = (codes, scales)
             codes, scales = codes_of[(unit, queries)]
             cols = slice(half * GROUP * P, (half + 1) * GROUP * P)
             nc.vector.quantize_mx(
                 out=codes[:, cols].bitcast(FP8X4), scales=scales[:, cols], in_=grouped_of[g][:]
             )
-            if part == 1:
+            if half == 1 and not queries:
                 split = k_split[unit % 2]
                 nc.sync.dma_start(out=split[0 : P // 2, 0, :].bitcast(I32), in_=codes[0 : P // 2, :].bitcast(I32))
                 nc.sync.dma_start(out=split[P // 2 : P, 1, :].bitcast(I32), in_=codes[P // 2 : P, :].bitcast(I32))
@@ -191,7 +198,7 @@ def tile_slidingwindowattention_pa_t_kernel(tc, x, Wqk, out):
         def scores(g):
             if not is_queries(g):
                 return
-            unit, rh = g // UNIT_GROUPS, g % 2
+            unit, rh = order[g][0], order[g][2]
             q_codes, q_scales = codes_of[(unit, 1)]
             k_scales = codes_of[(unit, 0)][1]
             split = k_split[unit % 2]
@@ -239,7 +246,7 @@ def tile_slidingwindowattention_pa_t_kernel(tc, x, Wqk, out):
         def normalise_and_store(g):
             if not is_queries(g):
                 return
-            unit, rh = g // UNIT_GROUPS, g % 2
+            unit, rh = order[g][0], order[g][2]
             weights = weights_of[g]
             inverse = soft.tile([P, 2], F32)
             nc.vector.reciprocal(out=inverse[:], in_=row_sum_of[g][:])
@@ -279,7 +286,8 @@ def tile_slidingwindowattention_pa_t_kernel(tc, x, Wqk, out):
                     scores(g - SCORE_LAG)
                     exponentials(g - SCORE_LAG - 1)
                 if i == 1:
-                    quantise(g - 1)
                     row_max(g - SCORE_LAG)
+                if i == 2:
+                    quantise(g - 1)
                 if i == GROUP - 1:
                     normalise_and_store(g - SCORE_LAG - 1)

@@ -139,6 +139,7 @@ def tile_slidingwindowattention_pa_t_kernel(tc, x, Wqk, out):
         minus_max_of = {}
         weights_of = {}
         row_sum_of = {}
+        inverse_of = {}
 
         order = []
         for r in range(UNITS + 1):
@@ -170,11 +171,16 @@ def tile_slidingwindowattention_pa_t_kernel(tc, x, Wqk, out):
             )
             dst = grouped_of[g][:, i * CHUNK : (i + 1) * CHUNK].rearrange("p (w j) -> p w j", j=PACK)
             src = acc[:].rearrange("p (j w) -> p w j", j=PACK)
-            factor = QUERY_FACTOR if queries else 1.0
             if on_vector(g * GROUP + i):
-                nc.vector.tensor_scalar_mul(out=dst, in0=src, scalar1=factor)
+                if queries:
+                    nc.vector.tensor_scalar_mul(out=dst, in0=src, scalar1=QUERY_FACTOR)
+                else:
+                    nc.vector.tensor_copy(out=dst, in_=src)
             else:
-                nc.scalar.activation(out=dst, in_=src, func=ACT.Copy, scale=factor)
+                if queries:
+                    nc.scalar.activation(out=dst, in_=src, func=ACT.Copy, scale=QUERY_FACTOR)
+                else:
+                    nc.scalar.copy(out=dst, in_=src)
 
         def quantise(g):
             if not 0 <= g < GROUPS:
@@ -243,13 +249,19 @@ def tile_slidingwindowattention_pa_t_kernel(tc, x, Wqk, out):
             weights_of[g] = weights
             row_sum_of[g] = row_sum
 
+        def invert_sums(g):
+            if not is_queries(g):
+                return
+            inverse = soft.tile([P, 2], F32)
+            nc.vector.reciprocal(out=inverse[:], in_=row_sum_of[g][:])
+            inverse_of[g] = inverse
+
         def normalise_and_store(g):
             if not is_queries(g):
                 return
             unit, rh = order[g][0], order[g][2]
             weights = weights_of[g]
-            inverse = soft.tile([P, 2], F32)
-            nc.vector.reciprocal(out=inverse[:], in_=row_sum_of[g][:])
+            inverse = inverse_of[g]
             for h in range(2):
                 nc.vector.tensor_scalar_mul(
                     out=weights[:, h, :], in0=weights[:, h, :], scalar1=inverse[:, h : h + 1]
@@ -288,6 +300,7 @@ def tile_slidingwindowattention_pa_t_kernel(tc, x, Wqk, out):
                 if i == 1:
                     row_max(g - SCORE_LAG)
                 if i == 2:
+                    invert_sums(g - SCORE_LAG - 1)
                     quantise(g - 1)
                 if i == GROUP - 1:
                     normalise_and_store(g - SCORE_LAG - 1)

@@ -28,7 +28,7 @@ GROUP = 4
 UNIT_GROUPS = 4
 GROUPS = UNITS * UNIT_GROUPS
 UNIT_WORDS = J_GROUPS * ROWS
-VECTOR_EVERY = 3
+W_GROUPS = (1, 2, 3, 4)
 TURN_AHEAD = 3
 SCORE_LAG = 3
 DRAIN = SCORE_LAG + 2
@@ -41,7 +41,7 @@ def tile_slidingwindowattention_pa_t_kernel(tc, x, Wqk, out):
     with ExitStack() as ctx:
         keep = ctx.enter_context(tc.tile_pool(name="keep", bufs=1))
         x_pool = ctx.enter_context(tc.tile_pool(name="x_pool", bufs=BATCH * CHUNKS))
-        w_pool = ctx.enter_context(tc.tile_pool(name="w_pool", bufs=PAIRS))
+        w_pool = ctx.enter_context(tc.tile_pool(name="w_pool", bufs=PAIRS + 1))
         stage = ctx.enter_context(tc.tile_pool(name="stage", bufs=3))
         g_pool = ctx.enter_context(tc.tile_pool(name="g_pool", bufs=4))
         k_pool = ctx.enter_context(tc.tile_pool(name="k_pool", bufs=3))
@@ -51,28 +51,42 @@ def tile_slidingwindowattention_pa_t_kernel(tc, x, Wqk, out):
         score_psum = ctx.enter_context(tc.psum_pool(name="score_psum", bufs=2))
         ctx.enter_context(tc.manual_schedule())
 
-        w_view = Wqk.rearrange("(s hp p) d -> hp p s d", s=2, hp=PAIRS, p=P)
         x_view = x.rearrange(
             "b (rh w jg jj) d -> b jg rh w (jj d)", rh=ROW_HALVES, w=P, jg=J_GROUPS, jj=PACK
         )
-        w_raw = {}
+        w_sets = [[(0, 0)]] + [[(hp, 0), (hp - 1, 1)] for hp in range(1, PAIRS)] + [[(PAIRS - 1, 1)]]
+        w_place = {}
+        for w_set in w_sets:
+            for block in w_set:
+                w_place[block] = len(w_place)
+        w_raw = []
         x_raw = {}
 
-        def load_w(hp):
+        def load_w(w_set):
             w_tile = w_pool.tile([P, 2 * MODEL], BF16)
-            nc.sync.dma_start(out=w_tile[:].rearrange("p (s d) -> p s d", s=2), in_=w_view[hp])
-            w_raw[hp] = w_tile
+            for n, (hp, queries) in enumerate(w_set):
+                first_row = ((1 - queries) * PAIRS + hp) * P
+                nc.sync.dma_start(
+                    out=w_tile[:, n * MODEL : (n + 1) * MODEL], in_=Wqk[first_row : first_row + P, :]
+                )
+            w_raw.append(w_tile)
 
         def load_x(b, c):
             x_tile = x_pool.tile([P, PACK * MODEL], BF16)
-            nc.sync.dma_start(out=x_tile[:], in_=x_view[b, c // ROW_HALVES, c % ROW_HALVES])
+            src = x_view[b, c // ROW_HALVES, c % ROW_HALVES]
+            parts = 2 if (b, c) == (0, 0) else 1
+            width = PACK * MODEL // parts
+            for n in range(parts):
+                nc.sync.dma_start(
+                    out=x_tile[:, n * width : (n + 1) * width], in_=src[:, n * width : (n + 1) * width]
+                )
             x_raw[(b, c)] = x_tile
 
-        load_w(0)
+        load_w(w_sets[0])
         for c in range(CHUNKS):
             load_x(0, c)
-        for hp in range(1, PAIRS):
-            load_w(hp)
+        for w_set in w_sets[1:]:
+            load_w(w_set)
 
         ident = keep.tile([P, P], F32)
         make_identity(nc, ident[:])
@@ -91,15 +105,13 @@ def tile_slidingwindowattention_pa_t_kernel(tc, x, Wqk, out):
             nc.vector.memset(k_split_tile[:].bitcast(I32), 0)
             k_split.append(k_split_tile)
 
-        def on_vector(bank_number):
-            return bank_number % VECTOR_EVERY == VECTOR_EVERY - 1
-
-        def turn(raw, pieces, grouped, first_bank):
+        def turn(raw, pieces, grouped):
             raw_words = raw[:].bitcast(F32)
             grouped_words = grouped[:].bitcast(F32).rearrange("p (n r u) -> p n r u", r=P, u=2)
-            for bank in range(pieces // 2):
+            for bank in range((pieces + 1) // 2):
+                inside = min(2, pieces - 2 * bank)
                 turned = bank_psum.tile([P, 2 * 2 * P], F32, tag="bank")
-                for n in range(2):
+                for n in range(inside):
                     for u in range(2):
                         first = (2 * bank + n) * WORDS + u * P
                         nc.tensor.transpose(
@@ -107,24 +119,29 @@ def tile_slidingwindowattention_pa_t_kernel(tc, x, Wqk, out):
                             raw_words[:, first : first + P],
                             ident[:],
                         )
-                dst = grouped_words[:, 2 * bank : 2 * bank + 2, :, :]
-                src = turned[:].rearrange("p (n u r) -> p n r u", n=2, u=2)
-                if on_vector(first_bank + bank):
+                dst = grouped_words[:, 2 * bank : 2 * bank + inside, :, :]
+                src = turned[:, : inside * 2 * P].rearrange("p (n u r) -> p n r u", n=inside, u=2)
+                if bank == 1:
                     nc.vector.tensor_copy(out=dst, in_=src)
                 else:
                     nc.scalar.copy(out=dst, in_=src)
 
-        def prepare_w(hp):
+        def turn_w(n):
             w_grouped = stage.tile([P, 2 * P * PACK], BF16, align_bytes=64)
-            turn(w_raw[hp], 2, w_grouped, hp)
-            cols = slice(hp * 2 * P, (hp + 1) * 2 * P)
+            turn(w_raw[n], len(w_sets[n]), w_grouped)
+            return n, w_grouped
+
+        def quantise_w(n, w_grouped):
+            first = w_place[w_sets[n][0]] * P
+            width = len(w_sets[n]) * P
+            cols = slice(first, first + width)
             nc.vector.quantize_mx(
-                out=w_codes[:, cols].bitcast(FP8X4), scales=w_scales[:, cols], in_=w_grouped[:]
+                out=w_codes[:, cols].bitcast(FP8X4), scales=w_scales[:, cols], in_=w_grouped[:, : width * PACK]
             )
 
         def turn_x(b, c):
             x_grouped = stage.tile([P, CHUNK * PACK], BF16, align_bytes=64)
-            turn(x_raw[(b, c)], PACK, x_grouped, (b * CHUNKS + c) * 2)
+            turn(x_raw[(b, c)], PACK, x_grouped)
             return b, c, x_grouped
 
         def quantise_x(b, c, x_grouped):
@@ -136,6 +153,7 @@ def tile_slidingwindowattention_pa_t_kernel(tc, x, Wqk, out):
         grouped_of = {}
         codes_of = {}
         score_of = {}
+        both_of = {}
         minus_max_of = {}
         weights_of = {}
         row_sum_of = {}
@@ -143,13 +161,21 @@ def tile_slidingwindowattention_pa_t_kernel(tc, x, Wqk, out):
 
         order = []
         for r in range(UNITS + 1):
-            if r < UNITS:
-                order.extend([(r, 0, 0), (r, 0, 1)])
-            if r >= 1:
-                order.extend([(r - 1, 1, 0), (r - 1, 1, 1)])
+            for half in range(2):
+                if r < UNITS:
+                    order.append((r, 0, half))
+                if r >= 1:
+                    order.append((r - 1, 1, half))
 
         def is_queries(g):
             return 0 <= g < GROUPS and order[g][1] == 1
+
+        def on_vector(g, i):
+            if g < 2:
+                return False
+            if UNIT_GROUPS <= g < UNIT_GROUPS + CHUNKS:
+                return i == 2
+            return i == 2 or (i == 0 and (g % 4 == 2 or g < UNIT_GROUPS))
 
         def project(g, i):
             unit, queries, half = order[g]
@@ -157,7 +183,8 @@ def tile_slidingwindowattention_pa_t_kernel(tc, x, Wqk, out):
             if i == 0:
                 grouped_of[g] = g_pool.tile([P, GROUP * CHUNK], BF16, name="grouped", align_bytes=64)
             c = i * ROW_HALVES + half if queries else half * GROUP + i
-            w_cols = slice((hp * 2 + 1 - queries) * P, (hp * 2 + 2 - queries) * P)
+            w_first = w_place[(hp, queries)] * P
+            w_cols = slice(w_first, w_first + P)
             x_cols = slice((b * CHUNKS + c) * CHUNK, (b * CHUNKS + c + 1) * CHUNK)
             acc = bank_psum.tile([P, CHUNK], F32, tag="bank")
             nc.tensor.matmul_mx(
@@ -171,7 +198,7 @@ def tile_slidingwindowattention_pa_t_kernel(tc, x, Wqk, out):
             )
             dst = grouped_of[g][:, i * CHUNK : (i + 1) * CHUNK].rearrange("p (w j) -> p w j", j=PACK)
             src = acc[:].rearrange("p (j w) -> p w j", j=PACK)
-            if on_vector(g * GROUP + i):
+            if on_vector(g, i):
                 if queries:
                     nc.vector.tensor_scalar_mul(out=dst, in0=src, scalar1=QUERY_FACTOR)
                 else:
@@ -182,72 +209,83 @@ def tile_slidingwindowattention_pa_t_kernel(tc, x, Wqk, out):
                 else:
                     nc.scalar.copy(out=dst, in_=src)
 
-        def quantise(g):
+        def quantise(g, part=0):
             if not 0 <= g < GROUPS:
                 return
             unit, queries, half = order[g]
+            parts = 2 if g == GROUPS - 1 else 1
             if half == 0:
                 pool = q_pool if queries else k_pool
                 codes = pool.tile([P, UNIT_WORDS], U32, name="codes", align_bytes=64)
                 scales = pool.tile([P, UNIT_WORDS], U8, name="scales", align_bytes=64)
                 codes_of[(unit, queries)] = (codes, scales)
             codes, scales = codes_of[(unit, queries)]
-            cols = slice(half * GROUP * P, (half + 1) * GROUP * P)
+            width = GROUP * P // parts
+            first = half * GROUP * P + part * width
+            cols = slice(first, first + width)
             nc.vector.quantize_mx(
-                out=codes[:, cols].bitcast(FP8X4), scales=scales[:, cols], in_=grouped_of[g][:]
+                out=codes[:, cols].bitcast(FP8X4),
+                scales=scales[:, cols],
+                in_=grouped_of[g][:, part * width * PACK : (part + 1) * width * PACK],
             )
             if half == 1 and not queries:
                 split = k_split[unit % 2]
                 nc.sync.dma_start(out=split[0 : P // 2, 0, :].bitcast(I32), in_=codes[0 : P // 2, :].bitcast(I32))
                 nc.sync.dma_start(out=split[P // 2 : P, 1, :].bitcast(I32), in_=codes[P // 2 : P, :].bitcast(I32))
 
-        def scores(g):
-            if not is_queries(g):
-                return
+        def score_passes(g, h, jgs):
             unit, rh = order[g][0], order[g][2]
             q_codes, q_scales = codes_of[(unit, 1)]
             k_scales = codes_of[(unit, 0)][1]
             split = k_split[unit % 2]
-            score = score_psum.tile([P, 2, ROWS], F32)
-            for h in range(2):
-                for jg in range(J_GROUPS):
-                    q_cols = slice((rh * J_GROUPS + jg) * P, (rh * J_GROUPS + jg + 1) * P)
-                    k_cols = slice(jg * ROWS, (jg + 1) * ROWS)
-                    nc.tensor.matmul_mx(
-                        out=score[:, h, :],
-                        lhsT=q_codes[:, q_cols].bitcast(FP8X4),
-                        lhsT_scale=q_scales[:, q_cols],
-                        rhs=split[:, h, k_cols].bitcast(FP8X4),
-                        rhs_scale=k_scales[:, k_cols],
-                        start=(jg == 0),
-                        stop=(jg == J_GROUPS - 1),
-                    )
-            score_of[g] = score
+            for jg in jgs:
+                q_cols = slice((rh * J_GROUPS + jg) * P, (rh * J_GROUPS + jg + 1) * P)
+                k_cols = slice(jg * ROWS, (jg + 1) * ROWS)
+                nc.tensor.matmul_mx(
+                    out=score_of[(g, h)],
+                    lhsT=q_codes[:, q_cols].bitcast(FP8X4),
+                    lhsT_scale=q_scales[:, q_cols],
+                    rhs=split[:, h, k_cols].bitcast(FP8X4),
+                    rhs_scale=k_scales[:, k_cols],
+                    start=(jg == 0),
+                    stop=(jg == J_GROUPS - 1),
+                )
+
+        def scores(g, i):
+            if not is_queries(g):
+                return
+            if i == 0:
+                score = score_psum.tile([P, 2, ROWS], F32, name="score")
+                both_of[g] = score
+                for h in range(2):
+                    score_of[(g, h)] = score[:, h, :]
+            score_passes(g, i // 2, range(i % 2 * 2, i % 2 * 2 + 2))
 
         def row_max(g):
             if not is_queries(g):
                 return
             minus_max = soft.tile([P, 2], F32)
             nc.vector.tensor_reduce(
-                out=minus_max[:], in_=score_of[g][:], axis=mybir.AxisListType.X, op=mybir.AluOpType.max, negate=True
+                out=minus_max[:], in_=both_of[g][:], axis=mybir.AxisListType.X, op=mybir.AluOpType.max, negate=True
             )
             minus_max_of[g] = minus_max
 
         def exponentials(g):
             if not is_queries(g):
                 return
-            weights = soft.tile([P, 2, ROWS], F32)
-            row_sum = soft.tile([P, 2], F32)
+            weights_of[g] = soft.tile([P, 2, ROWS], F32, name="weights")
+            row_sum_of[g] = soft.tile([P, 2], F32, name="row_sum")
             for h in range(2):
-                nc.scalar.activation(
-                    out=weights[:, h, :],
-                    in_=score_of[g][:, h, :],
-                    func=ACT.Exp,
-                    bias=minus_max_of[g][:, h : h + 1],
-                    accum_out=row_sum[:, h : h + 1],
-                )
-            weights_of[g] = weights
-            row_sum_of[g] = row_sum
+                exponential(g, h)
+
+        def exponential(g, h):
+            nc.scalar.activation(
+                out=weights_of[g][:, h, :],
+                in_=score_of[(g, h)],
+                func=ACT.Exp,
+                bias=minus_max_of[g][:, h : h + 1],
+                accum_out=row_sum_of[g][:, h : h + 1],
+            )
 
         def invert_sums(g):
             if not is_queries(g):
@@ -261,23 +299,26 @@ def tile_slidingwindowattention_pa_t_kernel(tc, x, Wqk, out):
                 return
             unit, rh = order[g][0], order[g][2]
             weights = weights_of[g]
-            inverse = inverse_of[g]
             for h in range(2):
                 nc.vector.tensor_scalar_mul(
-                    out=weights[:, h, :], in0=weights[:, h, :], scalar1=inverse[:, h : h + 1]
+                    out=weights[:, h, :], in0=weights[:, h, :], scalar1=inverse_of[g][:, h : h + 1]
                 )
             nc.sync.dma_start(
                 out=out[unit * 2 : unit * 2 + 2, rh * P : (rh + 1) * P, :].rearrange("h w c -> w h c"),
                 in_=weights[:],
             )
 
-        prepare_w(0)
+        quantise_w(*turn_w(0))
         turned = None
         for c in range(TURN_AHEAD):
             if turned:
                 quantise_x(*turned)
             turned = turn_x(0, c)
-        for g in range(GROUPS + DRAIN):
+        turned_w = None
+        for g in range(GROUPS):
+            last = g == GROUPS - 1
+            scored = g - SCORE_LAG + last
+            softened = g - SCORE_LAG - 1
             for i in range(GROUP):
                 step = g * GROUP + i
                 if i == 0 and g < CHUNKS:
@@ -290,17 +331,63 @@ def tile_slidingwindowattention_pa_t_kernel(tc, x, Wqk, out):
                     turned = turn_x(1, g - UNIT_GROUPS)
                 if before:
                     quantise_x(*before)
-                if i == 2 and 1 <= g < PAIRS:
-                    prepare_w(g)
-                if g < GROUPS:
-                    project(g, i)
+                if turned_w:
+                    quantise_w(*turned_w)
+                    turned_w = None
+                if i == 2 and g in W_GROUPS:
+                    turned_w = turn_w(1 + W_GROUPS.index(g))
+                project(g, i)
+                if not last:
+                    scores(scored, i)
                 if i == 0:
-                    scores(g - SCORE_LAG)
-                    exponentials(g - SCORE_LAG - 1)
+                    row_max(softened)
+                    invert_sums(softened - 1)
                 if i == 1:
-                    row_max(g - SCORE_LAG)
+                    exponentials(softened)
                 if i == 2:
-                    invert_sums(g - SCORE_LAG - 1)
                     quantise(g - 1)
-                if i == GROUP - 1:
-                    normalise_and_store(g - SCORE_LAG - 1)
+                if i == 3:
+                    normalise_and_store(softened - 1)
+
+        final = GROUPS - 1
+        quantise(final, 0)
+        invert_sums(final - 4)
+        normalise_and_store(final - 4)
+        for g in (final - 2, final - 1):
+            for i in range(GROUP):
+                scores(g, i)
+        row_max(final - 2)
+        exponentials(final - 2)
+        quantise(final, 1)
+        for h in range(2):
+            score_of[(final, h)] = bank_psum.tile([P, ROWS], F32, name="end", tag="bank")[:]
+        minus_max_of[final] = soft.tile([P, 2], F32, name="minus_max")
+        weights_of[final] = soft.tile([P, 2, ROWS], F32, name="weights")
+        row_sum_of[final] = soft.tile([P, 2], F32, name="row_sum")
+        inverse = soft.tile([P, 2], F32)
+        for jgs in ((0, 1), (2, 3)):
+            for h in range(2):
+                score_passes(final, h, jgs)
+        invert_sums(final - 2)
+        normalise_and_store(final - 2)
+        row_max(final - 1)
+        exponentials(final - 1)
+        for h in range(2):
+            nc.vector.tensor_reduce(
+                out=minus_max_of[final][:, h : h + 1],
+                in_=score_of[(final, h)],
+                axis=mybir.AxisListType.X,
+                op=mybir.AluOpType.max,
+                negate=True,
+            )
+            exponential(final, h)
+        invert_sums(final - 1)
+        normalise_and_store(final - 1)
+        unit, rh = order[final][0], order[final][2]
+        for h in range(2):
+            nc.vector.reciprocal(out=inverse[:, h : h + 1], in_=row_sum_of[final][:, h : h + 1])
+        for h in range(2):
+            nc.vector.tensor_scalar_mul(
+                out=weights_of[final][:, h, :], in0=weights_of[final][:, h, :], scalar1=inverse[:, h : h + 1]
+            )
+            nc.sync.dma_start(out=out[unit * 2 + h, rh * P : (rh + 1) * P, :], in_=weights_of[final][:, h, :])

@@ -28,7 +28,7 @@ GROUP = 4
 UNIT_GROUPS = 4
 GROUPS = UNITS * UNIT_GROUPS
 UNIT_WORDS = J_GROUPS * ROWS
-W_GROUPS = (1, 2, 3, 4)
+W_STEPS = (5, 13, 21, 29)
 TURN_AHEAD = 3
 SCORE_LAG = 3
 DRAIN = SCORE_LAG + 2
@@ -85,7 +85,9 @@ def tile_slidingwindowattention_pa_t_kernel(tc, x, Wqk, out):
         load_w(w_sets[0])
         for c in range(CHUNKS):
             load_x(0, c)
-        for w_set in w_sets[1:]:
+            if c == 3:
+                load_w(w_sets[1])
+        for w_set in w_sets[2:]:
             load_w(w_set)
 
         ident = keep.tile([P, P], F32)
@@ -175,7 +177,7 @@ def tile_slidingwindowattention_pa_t_kernel(tc, x, Wqk, out):
                 return False
             if UNIT_GROUPS <= g < UNIT_GROUPS + CHUNKS:
                 return i == 2
-            return i == 2 or (i == 0 and (g % 4 == 2 or g < UNIT_GROUPS))
+            return i == 2 or (i == 0 and (g % 4 == 2 or g < UNIT_GROUPS) and g < GROUPS - 2)
 
         def project(g, i):
             unit, queries, half = order[g]
@@ -334,44 +336,45 @@ def tile_slidingwindowattention_pa_t_kernel(tc, x, Wqk, out):
                 if turned_w:
                     quantise_w(*turned_w)
                     turned_w = None
-                if i == 2 and g in W_GROUPS:
-                    turned_w = turn_w(1 + W_GROUPS.index(g))
+                if step in W_STEPS:
+                    turned_w = turn_w(1 + W_STEPS.index(step))
                 project(g, i)
                 if not last:
                     scores(scored, i)
                 if i == 0:
                     row_max(softened)
                     invert_sums(softened - 1)
-                if i == 1:
+                if i == 1 and not last:
                     exponentials(softened)
-                if i == 2:
+                if i == 2 - last:
                     quantise(g - 1)
-                if i == 3:
+                if i == 3 and not last:
                     normalise_and_store(softened - 1)
 
         final = GROUPS - 1
-        quantise(final, 0)
-        invert_sums(final - 4)
-        normalise_and_store(final - 4)
         for g in (final - 2, final - 1):
             for i in range(GROUP):
                 scores(g, i)
-        row_max(final - 2)
-        exponentials(final - 2)
+        quantise(final, 0)
         quantise(final, 1)
+        exponentials(final - 4)
         for h in range(2):
             score_of[(final, h)] = bank_psum.tile([P, ROWS], F32, name="end", tag="bank")[:]
         minus_max_of[final] = soft.tile([P, 2], F32, name="minus_max")
         weights_of[final] = soft.tile([P, 2, ROWS], F32, name="weights")
         row_sum_of[final] = soft.tile([P, 2], F32, name="row_sum")
         inverse = soft.tile([P, 2], F32)
-        for jgs in ((0, 1), (2, 3)):
-            for h in range(2):
-                score_passes(final, h, jgs)
-        invert_sums(final - 2)
-        normalise_and_store(final - 2)
+        score_passes(final, 0, (0, 1))
+        score_passes(final, 1, (0, 1))
+        score_passes(final, 0, (2, 3))
+        score_passes(final, 1, (2, 3))
+        row_max(final - 2)
+        exponentials(final - 2)
+        invert_sums(final - 4)
         row_max(final - 1)
         exponentials(final - 1)
+        normalise_and_store(final - 4)
+        invert_sums(final - 2)
         for h in range(2):
             nc.vector.tensor_reduce(
                 out=minus_max_of[final][:, h : h + 1],
@@ -381,6 +384,7 @@ def tile_slidingwindowattention_pa_t_kernel(tc, x, Wqk, out):
                 negate=True,
             )
             exponential(final, h)
+        normalise_and_store(final - 2)
         invert_sums(final - 1)
         normalise_and_store(final - 1)
         unit, rh = order[final][0], order[final][2]

@@ -28,7 +28,9 @@ GROUP = 4
 UNIT_GROUPS = 4
 GROUPS = UNITS * UNIT_GROUPS
 UNIT_WORDS = J_GROUPS * ROWS
-W_STEPS = (5, 13, 21, 29)
+VECTOR_EVERY = 3
+W_GROUPS = (3, 4, 5)
+FIRST_TURN = 4
 TURN_AHEAD = 3
 SCORE_LAG = 3
 DRAIN = SCORE_LAG + 2
@@ -54,7 +56,7 @@ def tile_slidingwindowattention_pa_t_kernel(tc, x, Wqk, out):
         x_view = x.rearrange(
             "b (rh w jg jj) d -> b jg rh w (jj d)", rh=ROW_HALVES, w=P, jg=J_GROUPS, jj=PACK
         )
-        w_sets = [[(0, 0)]] + [[(hp, 0), (hp - 1, 1)] for hp in range(1, PAIRS)] + [[(PAIRS - 1, 1)]]
+        w_sets = [[(0, 0)], [(1, 0)], [(0, 1), (2, 0)], [(1, 1), (3, 0)], [(2, 1), (3, 1)]]
         w_place = {}
         for w_set in w_sets:
             for block in w_set:
@@ -83,10 +85,10 @@ def tile_slidingwindowattention_pa_t_kernel(tc, x, Wqk, out):
             x_raw[(b, c)] = x_tile
 
         load_w(w_sets[0])
-        for c in range(CHUNKS):
+        load_x(0, 0)
+        load_w(w_sets[1])
+        for c in range(1, CHUNKS):
             load_x(0, c)
-            if c == 3:
-                load_w(w_sets[1])
         for w_set in w_sets[2:]:
             load_w(w_set)
 
@@ -161,23 +163,28 @@ def tile_slidingwindowattention_pa_t_kernel(tc, x, Wqk, out):
         row_sum_of = {}
         inverse_of = {}
 
-        order = []
-        for r in range(UNITS + 1):
-            for half in range(2):
-                if r < UNITS:
-                    order.append((r, 0, half))
-                if r >= 1:
-                    order.append((r - 1, 1, half))
+        order = [(0, 0, 0), (1, 0, 0), (0, 0, 1), (1, 0, 1), (0, 1, 0), (0, 1, 1)]
+        for unit in range(1, UNITS):
+            for half in range(ROW_HALVES):
+                if unit + 1 < UNITS:
+                    order.append((unit + 1, 0, half))
+                order.append((unit, 1, half))
+        passes = []
+        for g in range(0, GROUPS, 2):
+            pair = [(g + n, i) for n in range(2) for i in range(GROUP)]
+            if g < UNIT_GROUPS:
+                pair = [(g + n, i) for i in range(GROUP) for n in range(2)]
+            passes.extend(pair)
 
         def is_queries(g):
             return 0 <= g < GROUPS and order[g][1] == 1
 
         def on_vector(g, i):
-            if g < 2:
+            if g < UNIT_GROUPS:
                 return False
-            if UNIT_GROUPS <= g < UNIT_GROUPS + CHUNKS:
+            if FIRST_TURN <= g < FIRST_TURN + CHUNKS:
                 return i == 2
-            return i == 2 or (i == 0 and (g % 4 == 2 or g < UNIT_GROUPS) and g < GROUPS - 2)
+            return i == 2 or (i == 0 and g % 4 == 2 and g < GROUPS - 2)
 
         def project(g, i):
             unit, queries, half = order[g]
@@ -257,7 +264,10 @@ def tile_slidingwindowattention_pa_t_kernel(tc, x, Wqk, out):
             if not is_queries(g):
                 return
             if i == 0:
-                score = score_psum.tile([P, 2, ROWS], F32, name="score")
+                if g == GROUPS - 2:
+                    score = bank_psum.tile([P, 2, ROWS], F32, name="score", tag="bank")
+                else:
+                    score = score_psum.tile([P, 2, ROWS], F32, name="score")
                 both_of[g] = score
                 for h in range(2):
                     score_of[(g, h)] = score[:, h, :]
@@ -310,35 +320,35 @@ def tile_slidingwindowattention_pa_t_kernel(tc, x, Wqk, out):
                 in_=weights[:],
             )
 
-        quantise_w(*turn_w(0))
-        turned = None
-        for c in range(TURN_AHEAD):
-            if turned:
-                quantise_x(*turned)
-            turned = turn_x(0, c)
+        first_w = turn_w(0)
+        first_x = turn_x(0, 0)
+        second_w = turn_w(1)
+        quantise_w(*first_w)
+        quantise_x(*first_x)
+        quantise_w(*second_w)
+        waiting = [turn_x(0, 1)]
         turned_w = None
         for g in range(GROUPS):
             last = g == GROUPS - 1
-            scored = g - SCORE_LAG + last
+            scored = g - SCORE_LAG
             softened = g - SCORE_LAG - 1
             for i in range(GROUP):
                 step = g * GROUP + i
-                if i == 0 and g < CHUNKS:
-                    load_x(1, g)
-                before = turned
-                turned = None
-                if step + TURN_AHEAD < CHUNKS:
-                    turned = turn_x(0, step + TURN_AHEAD)
-                elif i == 0 and UNIT_GROUPS <= g < UNIT_GROUPS + CHUNKS:
-                    turned = turn_x(1, g - UNIT_GROUPS)
+                if i == 0 and 1 <= g < 1 + CHUNKS:
+                    load_x(1, g - 1)
+                before = waiting.pop(0) if waiting and (g >= UNIT_GROUPS or step % 2 == 0) else None
+                if i == 0 and FIRST_TURN <= g < FIRST_TURN + CHUNKS:
+                    waiting.append(turn_x(1, g - FIRST_TURN))
                 if before:
                     quantise_x(*before)
                 if turned_w:
                     quantise_w(*turned_w)
                     turned_w = None
-                if step in W_STEPS:
-                    turned_w = turn_w(1 + W_STEPS.index(step))
-                project(g, i)
+                if i == 2 and g in W_GROUPS:
+                    turned_w = turn_w(2 + W_GROUPS.index(g))
+                project(*passes[step])
+                if step % 2 == 0 and step // 2 + 2 < CHUNKS:
+                    waiting.append(turn_x(0, step // 2 + 2))
                 if not last:
                     scores(scored, i)
                 if i == 0:
@@ -346,8 +356,9 @@ def tile_slidingwindowattention_pa_t_kernel(tc, x, Wqk, out):
                     invert_sums(softened - 1)
                 if i == 1 and not last:
                     exponentials(softened)
-                if i == 2 - last:
-                    quantise(g - 1)
+                done = step - 3 + last
+                if done >= 0 and passes[done][1] == GROUP - 1:
+                    quantise(passes[done][0])
                 if i == 3 and not last:
                     normalise_and_store(softened - 1)
 

@@ -109,9 +109,9 @@ def tile_slidingwindowattention_pa_t_kernel(tc, x, Wqk, out):
             nc.vector.memset(k_split_tile[:].bitcast(I32), 0)
             k_split.append(k_split_tile)
 
-        def turn(raw, pieces, grouped):
+        def turn(raw, pieces, grouped, by_row):
             raw_words = raw[:].bitcast(F32)
-            grouped_words = grouped[:].bitcast(F32).rearrange("p (n r u) -> p n r u", r=P, u=2)
+            grouped_words = grouped[:].bitcast(F32)
             for bank in range((pieces + 1) // 2):
                 inside = min(2, pieces - 2 * bank)
                 turned = bank_psum.tile([P, 2 * 2 * P], F32, tag="bank")
@@ -123,8 +123,12 @@ def tile_slidingwindowattention_pa_t_kernel(tc, x, Wqk, out):
                             raw_words[:, first : first + P],
                             ident[:],
                         )
-                dst = grouped_words[:, 2 * bank : 2 * bank + inside, :, :]
-                src = turned[:, : inside * 2 * P].rearrange("p (n u r) -> p n r u", n=inside, u=2)
+                if by_row:
+                    dst = grouped_words.rearrange("p (r k) -> p r k", r=P)[:, :, 4 * bank : 4 * bank + 4]
+                    src = turned[:].rearrange("p (k r) -> p r k", r=P)
+                else:
+                    dst = grouped_words[:, : inside * 2 * P].rearrange("p (n r u) -> p n r u", r=P, u=2)
+                    src = turned[:, : inside * 2 * P].rearrange("p (n u r) -> p n r u", r=P, u=2)
                 if bank == 1:
                     nc.vector.tensor_copy(out=dst, in_=src)
                 else:
@@ -132,7 +136,7 @@ def tile_slidingwindowattention_pa_t_kernel(tc, x, Wqk, out):
 
         def turn_w(n):
             w_grouped = stage.tile([P, 2 * P * PACK], BF16, align_bytes=64)
-            turn(w_raw[n], len(w_sets[n]), w_grouped)
+            turn(w_raw[n], len(w_sets[n]), w_grouped, False)
             return n, w_grouped
 
         def quantise_w(n, w_grouped):
@@ -145,7 +149,7 @@ def tile_slidingwindowattention_pa_t_kernel(tc, x, Wqk, out):
 
         def turn_x(b, c):
             x_grouped = stage.tile([P, CHUNK * PACK], BF16, align_bytes=64)
-            turn(x_raw[(b, c)], PACK, x_grouped)
+            turn(x_raw[(b, c)], PACK, x_grouped, True)
             return b, c, x_grouped
 
         def quantise_x(b, c, x_grouped):
@@ -205,8 +209,8 @@ def tile_slidingwindowattention_pa_t_kernel(tc, x, Wqk, out):
                 start=True,
                 stop=True,
             )
-            dst = grouped_of[g][:, i * CHUNK : (i + 1) * CHUNK].rearrange("p (w j) -> p w j", j=PACK)
-            src = acc[:].rearrange("p (j w) -> p w j", j=PACK)
+            dst = grouped_of[g][:, i * CHUNK : (i + 1) * CHUNK]
+            src = acc[:]
             if on_vector(g, i):
                 if queries:
                     nc.vector.tensor_scalar_mul(out=dst, in0=src, scalar1=QUERY_FACTOR)

@@ -185,7 +185,7 @@ def tile_slidingwindowattention_pa_t_kernel(tc, x, Wqk, out):
 
         def on_vector(g, i):
             if g < UNIT_GROUPS:
-                return False
+                return g % 2 == 1 and i == 2
             if FIRST_TURN <= g < FIRST_TURN + CHUNKS:
                 return i == 2
             return i == 2 or (i == 0 and g % 4 == 2 and g < GROUPS - 2)
@@ -226,8 +226,8 @@ def tile_slidingwindowattention_pa_t_kernel(tc, x, Wqk, out):
             if not 0 <= g < GROUPS:
                 return
             unit, queries, half = order[g]
-            parts = 2 if g == GROUPS - 1 else 1
-            if half == 0:
+            parts = 2
+            if half == 0 and part == 0:
                 pool = q_pool if queries else k_pool
                 codes = pool.tile([P, UNIT_WORDS], U32, name="codes", align_bytes=64)
                 scales = pool.tile([P, UNIT_WORDS], U8, name="scales", align_bytes=64)
@@ -241,7 +241,7 @@ def tile_slidingwindowattention_pa_t_kernel(tc, x, Wqk, out):
                 scales=scales[:, cols],
                 in_=grouped_of[g][:, part * width * PACK : (part + 1) * width * PACK],
             )
-            if half == 1 and not queries:
+            if half == 1 and part == 1 and not queries:
                 split = k_split[unit % 2]
                 nc.sync.dma_start(out=split[0 : P // 2, 0, :].bitcast(I32), in_=codes[0 : P // 2, :].bitcast(I32))
                 nc.sync.dma_start(out=split[P // 2 : P, 1, :].bitcast(I32), in_=codes[P // 2 : P, :].bitcast(I32))
@@ -360,9 +360,12 @@ def tile_slidingwindowattention_pa_t_kernel(tc, x, Wqk, out):
                     invert_sums(softened - 1)
                 if i == 1 and not last:
                     exponentials(softened)
-                done = step - 3 + last
-                if done >= 0 and passes[done][1] == GROUP - 1:
-                    quantise(passes[done][0])
+                for lag, place in ((3, 1), (3 - last, GROUP - 1)):
+                    if step < lag:
+                        continue
+                    done, at = passes[step - lag]
+                    if at == place:
+                        quantise(done, 1 if place == GROUP - 1 else 0)
                 if i == 3 and not last:
                     normalise_and_store(softened - 1)
 

@@ -42,13 +42,13 @@ def tile_slidingwindowattention_pa_t_kernel(tc, x, Wqk, out):
     nc = tc.nc
     with ExitStack() as ctx:
         keep = ctx.enter_context(tc.tile_pool(name="keep", bufs=1))
-        x_pool = ctx.enter_context(tc.tile_pool(name="x_pool", bufs=BATCH * CHUNKS))
+        x_pool = ctx.enter_context(tc.tile_pool(name="x_pool", bufs=CHUNKS))
         w_pool = ctx.enter_context(tc.tile_pool(name="w_pool", bufs=PAIRS + 1))
         stage = ctx.enter_context(tc.tile_pool(name="stage", bufs=3))
-        g_pool = ctx.enter_context(tc.tile_pool(name="g_pool", bufs=4))
-        k_pool = ctx.enter_context(tc.tile_pool(name="k_pool", bufs=3))
+        g_pool = ctx.enter_context(tc.tile_pool(name="g_pool", bufs=5))
+        k_pool = ctx.enter_context(tc.tile_pool(name="k_pool", bufs=UNITS))
         q_pool = ctx.enter_context(tc.tile_pool(name="q_pool", bufs=2))
-        soft = ctx.enter_context(tc.tile_pool(name="soft", bufs=4))
+        soft = ctx.enter_context(tc.tile_pool(name="soft", bufs=2 * UNITS))
         bank_psum = ctx.enter_context(tc.psum_pool(name="bank_psum", bufs=6))
         score_psum = ctx.enter_context(tc.psum_pool(name="score_psum", bufs=2))
         ctx.enter_context(tc.manual_schedule())
@@ -188,7 +188,7 @@ def tile_slidingwindowattention_pa_t_kernel(tc, x, Wqk, out):
                 return g % 2 == 1 and i == 2
             if FIRST_TURN <= g < FIRST_TURN + CHUNKS:
                 return i == 2
-            return i == 2 or (i == 0 and g % 4 == 2 and g < GROUPS - 2)
+            return i == 2 or (i == 0 and g % 4 == 2)
 
         def project(g, i):
             unit, queries, half = order[g]

from contextlib import ExitStack

import concourse.mybir as mybir
from concourse.masks import make_identity

F32 = mybir.dt.float32
BF16 = mybir.dt.bfloat16
I32 = mybir.dt.int32
U32 = mybir.dt.uint32
U8 = mybir.dt.uint8
FP8X4 = mybir.dt.float8_e4m3fn_x4
ACT = mybir.ActivationFunctionType

P = 128
PACK = 4
BATCH, TOKENS, MODEL = 2, 4096, 512
HEADS, HEAD_DIM, ROWS = 8, 64, 256
PER_ROW = TOKENS // ROWS
PAIRS = HEADS // 2
J_GROUPS = PER_ROW // PACK
ROW_HALVES = ROWS // P
CHUNKS = J_GROUPS * ROW_HALVES
CHUNK = P * PACK
WORDS = MODEL // 2
QUERY_FACTOR = HEAD_DIM ** -0.5
UNITS = BATCH * PAIRS
GROUP = 4
UNIT_GROUPS = 4
GROUPS = UNITS * UNIT_GROUPS
UNIT_WORDS = J_GROUPS * ROWS
VECTOR_EVERY = 3
W_GROUPS = (3, 4, 5)
FIRST_TURN = 4
TURN_AHEAD = 3
SCORE_LAG = 3
DRAIN = SCORE_LAG + 2

FLOPS = 2 * BATCH * TOKENS * MODEL * 2 * MODEL + 2 * BATCH * HEADS * ROWS * ROWS * PER_ROW * HEAD_DIM


def tile_slidingwindowattention_pa_t_kernel(tc, x, Wqk, out):
    nc = tc.nc
    with ExitStack() as ctx:
        keep = ctx.enter_context(tc.tile_pool(name="keep", bufs=1))
        x_pool = ctx.enter_context(tc.tile_pool(name="x_pool", bufs=CHUNKS))
        w_pool = ctx.enter_context(tc.tile_pool(name="w_pool", bufs=PAIRS + 1))
        stage = ctx.enter_context(tc.tile_pool(name="stage", bufs=3))
        g_pool = ctx.enter_context(tc.tile_pool(name="g_pool", bufs=5))
        k_pool = ctx.enter_context(tc.tile_pool(name="k_pool", bufs=UNITS))
        q_pool = ctx.enter_context(tc.tile_pool(name="q_pool", bufs=2))
        soft = ctx.enter_context(tc.tile_pool(name="soft", bufs=2 * UNITS))
        bank_psum = ctx.enter_context(tc.psum_pool(name="bank_psum", bufs=6))
        score_psum = ctx.enter_context(tc.psum_pool(name="score_psum", bufs=2))
        ctx.enter_context(tc.manual_schedule())

        x_view = x.rearrange(
            "b (rh w jg jj) d -> b jg rh w (jj d)", rh=ROW_HALVES, w=P, jg=J_GROUPS, jj=PACK
        )
        w_sets = [[(0, 0)], [(1, 0)], [(0, 1), (2, 0)], [(1, 1), (3, 0)], [(2, 1), (3, 1)]]
        w_place = {}
        for w_set in w_sets:
            for block in w_set:
                w_place[block] = len(w_place)
        w_raw = []
        x_raw = {}

        def load_w(w_set):
            w_tile = w_pool.tile([P, 2 * MODEL], BF16)
            for n, (hp, queries) in enumerate(w_set):
                first_row = ((1 - queries) * PAIRS + hp) * P
                nc.sync.dma_start(
                    out=w_tile[:, n * MODEL : (n + 1) * MODEL], in_=Wqk[first_row : first_row + P, :]
                )
            w_raw.append(w_tile)

        def load_x(b, c):
            x_tile = x_pool.tile([P, PACK * MODEL], BF16)
            src = x_view[b, c // ROW_HALVES, c % ROW_HALVES]
            parts = 2 if (b, c) == (0, 0) else 1
            width = PACK * MODEL // parts
            for n in range(parts):
                nc.sync.dma_start(
                    out=x_tile[:, n * width : (n + 1) * width], in_=src[:, n * width : (n + 1) * width]
                )
            x_raw[(b, c)] = x_tile

        load_w(w_sets[0])
        load_x(0, 0)
        load_w(w_sets[1])
        for c in range(1, CHUNKS):
            load_x(0, c)
        for w_set in w_sets[2:]:
            load_w(w_set)

        ident = keep.tile([P, P], F32)
        make_identity(nc, ident[:])
        warm_in = keep.tile([P, 1], F32)
        warm_out = keep.tile([P, 1], F32)
        nc.vector.memset(warm_in[:], 0.0)
        nc.scalar.activation(out=warm_out[:], in_=warm_in[:], func=ACT.Exp)

        w_codes = keep.tile([P, PAIRS * 2 * P], U32, align_bytes=64)
        w_scales = keep.tile([P, PAIRS * 2 * P], U8, align_bytes=64)
        x_codes = keep.tile([P, BATCH * CHUNKS * CHUNK], U32, align_bytes=64)
        x_scales = keep.tile([P, BATCH * CHUNKS * CHUNK], U8, align_bytes=64)
        k_split = []
        for parity in range(2):
            k_split_tile = keep.tile([P, 2, UNIT_WORDS], U32, name="k_split%d" % parity, align_bytes=64)
            nc.vector.memset(k_split_tile[:].bitcast(I32), 0)
            k_split.append(k_split_tile)

        def turn(raw, pieces, grouped, by_row):
            raw_words = raw[:].bitcast(F32)
            grouped_words = grouped[:].bitcast(F32)
            for bank in range((pieces + 1) // 2):
                inside = min(2, pieces - 2 * bank)
                turned = bank_psum.tile([P, 2 * 2 * P], F32, tag="bank")
                for n in range(inside):
                    for u in range(2):
                        first = (2 * bank + n) * WORDS + u * P
                        nc.tensor.transpose(
                            turned[:, (2 * n + u) * P : (2 * n + u + 1) * P],
                            raw_words[:, first : first + P],
                            ident[:],
                        )
                if by_row:
                    dst = grouped_words.rearrange("p (r k) -> p r k", r=P)[:, :, 4 * bank : 4 * bank + 4]
                    src = turned[:].rearrange("p (k r) -> p r k", r=P)
                else:
                    dst = grouped_words[:, : inside * 2 * P].rearrange("p (n r u) -> p n r u", r=P, u=2)
                    src = turned[:, : inside * 2 * P].rearrange("p (n u r) -> p n r u", r=P, u=2)
                if bank == 1:
                    nc.vector.tensor_copy(out=dst, in_=src)
                else:
                    nc.scalar.copy(out=dst, in_=src)

        def turn_w(n):
            w_grouped = stage.tile([P, 2 * P * PACK], BF16, align_bytes=64)
            turn(w_raw[n], len(w_sets[n]), w_grouped, False)
            return n, w_grouped

        def quantise_w(n, w_grouped):
            first = w_place[w_sets[n][0]] * P
            width = len(w_sets[n]) * P
            cols = slice(first, first + width)
            nc.vector.quantize_mx(
                out=w_codes[:, cols].bitcast(FP8X4), scales=w_scales[:, cols], in_=w_grouped[:, : width * PACK]
            )

        def turn_x(b, c):
            x_grouped = stage.tile([P, CHUNK * PACK], BF16, align_bytes=64)
            turn(x_raw[(b, c)], PACK, x_grouped, True)
            return b, c, x_grouped

        def quantise_x(b, c, x_grouped):
            cols = slice((b * CHUNKS + c) * CHUNK, (b * CHUNKS + c + 1) * CHUNK)
            nc.vector.quantize_mx(
                out=x_codes[:, cols].bitcast(FP8X4), scales=x_scales[:, cols], in_=x_grouped[:]
            )

        grouped_of = {}
        codes_of = {}
        score_of = {}
        both_of = {}
        minus_max_of = {}
        weights_of = {}
        row_sum_of = {}
        inverse_of = {}

        order = [(0, 0, 0), (1, 0, 0), (0, 0, 1), (1, 0, 1), (0, 1, 0), (0, 1, 1)]
        for unit in range(1, UNITS):
            for half in range(ROW_HALVES):
                if unit + 1 < UNITS:
                    order.append((unit + 1, 0, half))
                order.append((unit, 1, half))
        passes = []
        for g in range(0, GROUPS, 2):
            pair = [(g + n, i) for n in range(2) for i in range(GROUP)]
            if g < UNIT_GROUPS:
                pair = [(g + n, i) for i in range(GROUP) for n in range(2)]
            passes.extend(pair)

        def is_queries(g):
            return 0 <= g < GROUPS and order[g][1] == 1

        def on_vector(g, i):
            if g < UNIT_GROUPS:
                return g % 2 == 1 and i == 2
            if FIRST_TURN <= g < FIRST_TURN + CHUNKS:
                return i == 2
            return i == 2 or (i == 0 and g % 4 == 2)

        def project(g, i):
            unit, queries, half = order[g]
            b, hp = divmod(unit, PAIRS)
            if i == 0:
                grouped_of[g] = g_pool.tile([P, GROUP * CHUNK], BF16, name="grouped", align_bytes=64)
            c = i * ROW_HALVES + half if queries else half * GROUP + i
            w_first = w_place[(hp, queries)] * P
            w_cols = slice(w_first, w_first + P)
            x_cols = slice((b * CHUNKS + c) * CHUNK, (b * CHUNKS + c + 1) * CHUNK)
            acc = bank_psum.tile([P, CHUNK], F32, tag="bank")
            nc.tensor.matmul_mx(
                out=acc[:],
                lhsT=w_codes[:, w_cols].bitcast(FP8X4),
                lhsT_scale=w_scales[:, w_cols],
                rhs=x_codes[:, x_cols].bitcast(FP8X4),
                rhs_scale=x_scales[:, x_cols],
                start=True,
                stop=True,
            )
            dst = grouped_of[g][:, i * CHUNK : (i + 1) * CHUNK]
            src = acc[:]
            if on_vector(g, i):
                if queries:
                    nc.vector.tensor_scalar_mul(out=dst, in0=src, scalar1=QUERY_FACTOR)
                else:
                    nc.vector.tensor_copy(out=dst, in_=src)
            else:
                if queries:
                    nc.scalar.activation(out=dst, in_=src, func=ACT.Copy, scale=QUERY_FACTOR)
                else:
                    nc.scalar.copy(out=dst, in_=src)

        def quantise(g, part=0):
            if not 0 <= g < GROUPS:
                return
            unit, queries, half = order[g]
            parts = 2
            if half == 0 and part == 0:
                pool = q_pool if queries else k_pool
                codes = pool.tile([P, UNIT_WORDS], U32, name="codes", align_bytes=64)
                scales = pool.tile([P, UNIT_WORDS], U8, name="scales", align_bytes=64)
                codes_of[(unit, queries)] = (codes, scales)
            codes, scales = codes_of[(unit, queries)]
            width = GROUP * P // parts
            first = half * GROUP * P + part * width
            cols = slice(first, first + width)
            nc.vector.quantize_mx(
                out=codes[:, cols].bitcast(FP8X4),
                scales=scales[:, cols],
                in_=grouped_of[g][:, part * width * PACK : (part + 1) * width * PACK],
            )
            if half == 1 and part == 1 and not queries:
                split = k_split[unit % 2]
                nc.sync.dma_start(out=split[0 : P // 2, 0, :].bitcast(I32), in_=codes[0 : P // 2, :].bitcast(I32))
                nc.sync.dma_start(out=split[P // 2 : P, 1, :].bitcast(I32), in_=codes[P // 2 : P, :].bitcast(I32))

        def score_passes(g, h, jgs):
            unit, rh = order[g][0], order[g][2]
            q_codes, q_scales = codes_of[(unit, 1)]
            k_scales = codes_of[(unit, 0)][1]
            split = k_split[unit % 2]
            for jg in jgs:
                q_cols = slice((rh * J_GROUPS + jg) * P, (rh * J_GROUPS + jg + 1) * P)
                k_cols = slice(jg * ROWS, (jg + 1) * ROWS)
                nc.tensor.matmul_mx(
                    out=score_of[(g, h)],
                    lhsT=q_codes[:, q_cols].bitcast(FP8X4),
                    lhsT_scale=q_scales[:, q_cols],
                    rhs=split[:, h, k_cols].bitcast(FP8X4),
                    rhs_scale=k_scales[:, k_cols],
                    start=(jg == 0),
                    stop=(jg == J_GROUPS - 1),
                )

        def scores(g, i):
            if not is_queries(g):
                return
            if i == 0:
                if g == GROUPS - 2:
                    score = bank_psum.tile([P, 2, ROWS], F32, name="score", tag="bank")
                else:
                    score = score_psum.tile([P, 2, ROWS], F32, name="score")
                both_of[g] = score
                for h in range(2):
                    score_of[(g, h)] = score[:, h, :]
            score_passes(g, i // 2, range(i % 2 * 2, i % 2 * 2 + 2))

        def row_max(g):
            if not is_queries(g):
                return
            minus_max = soft.tile([P, 2], F32)
            nc.vector.tensor_reduce(
                out=minus_max[:], in_=both_of[g][:], axis=mybir.AxisListType.X, op=mybir.AluOpType.max, negate=True
            )
            minus_max_of[g] = minus_max

        def exponentials(g):
            if not is_queries(g):
                return
            weights_of[g] = soft.tile([P, 2, ROWS], F32, name="weights")
            row_sum_of[g] = soft.tile([P, 2], F32, name="row_sum")
            for h in range(2):
                exponential(g, h)

        def exponential(g, h):
            nc.scalar.activation(
                out=weights_of[g][:, h, :],
                in_=score_of[(g, h)],
                func=ACT.Exp,
                bias=minus_max_of[g][:, h : h + 1],
                accum_out=row_sum_of[g][:, h : h + 1],
            )

        def invert_sums(g):
            if not is_queries(g):
                return
            inverse = soft.tile([P, 2], F32)
            nc.vector.reciprocal(out=inverse[:], in_=row_sum_of[g][:])
            inverse_of[g] = inverse

        def normalise_and_store(g):
            if not is_queries(g):
                return
            unit, rh = order[g][0], order[g][2]
            weights = weights_of[g]
            for h in range(2):
                nc.vector.tensor_scalar_mul(
                    out=weights[:, h, :], in0=weights[:, h, :], scalar1=inverse_of[g][:, h : h + 1]
                )
            nc.sync.dma_start(
                out=out[unit * 2 : unit * 2 + 2, rh * P : (rh + 1) * P, :].rearrange("h w c -> w h c"),
                in_=weights[:],
            )

        first_w = turn_w(0)
        first_x = turn_x(0, 0)
        second_w = turn_w(1)
        quantise_w(*first_w)
        quantise_x(*first_x)
        quantise_w(*second_w)
        waiting = [turn_x(0, 1)]
        turned_w = None
        for g in range(GROUPS):
            last = g == GROUPS - 1
            scored = g - SCORE_LAG
            softened = g - SCORE_LAG - 1
            for i in range(GROUP):
                step = g * GROUP + i
                if i == 0 and 1 <= g < 1 + CHUNKS:
                    load_x(1, g - 1)
                before = waiting.pop(0) if waiting and (g >= UNIT_GROUPS or step % 2 == 0) else None
                if i == 0 and FIRST_TURN <= g < FIRST_TURN + CHUNKS:
                    waiting.append(turn_x(1, g - FIRST_TURN))
                if before:
                    quantise_x(*before)
                if turned_w:
                    quantise_w(*turned_w)
                    turned_w = None
                if i == 2 and g in W_GROUPS:
                    turned_w = turn_w(2 + W_GROUPS.index(g))
                project(*passes[step])
                if step % 2 == 0 and step // 2 + 2 < CHUNKS:
                    waiting.append(turn_x(0, step // 2 + 2))
                if not last:
                    scores(scored, i)
                if i == 0:
                    row_max(softened)
                    invert_sums(softened - 1)
                if i == 1 and not last:
                    exponentials(softened)
                for lag, place in ((3, 1), (3 - last, GROUP - 1)):
                    if step < lag:
                        continue
                    done, at = passes[step - lag]
                    if at == place:
                        quantise(done, 1 if place == GROUP - 1 else 0)
                if i == 3 and not last:
                    normalise_and_store(softened - 1)

        final = GROUPS - 1
        for g in (final - 2, final - 1):
            for i in range(GROUP):
                scores(g, i)
        quantise(final, 0)
        quantise(final, 1)
        exponentials(final - 4)
        for h in range(2):
            score_of[(final, h)] = bank_psum.tile([P, ROWS], F32, name="end", tag="bank")[:]
        minus_max_of[final] = soft.tile([P, 2], F32, name="minus_max")
        weights_of[final] = soft.tile([P, 2, ROWS], F32, name="weights")
        row_sum_of[final] = soft.tile([P, 2], F32, name="row_sum")
        inverse = soft.tile([P, 2], F32)
        score_passes(final, 0, (0, 1))
        score_passes(final, 1, (0, 1))
        score_passes(final, 0, (2, 3))
        score_passes(final, 1, (2, 3))
        row_max(final - 2)
        exponentials(final - 2)
        invert_sums(final - 4)
        row_max(final - 1)
        exponentials(final - 1)
        normalise_and_store(final - 4)
        invert_sums(final - 2)
        for h in range(2):
            nc.vector.tensor_reduce(
                out=minus_max_of[final][:, h : h + 1],
                in_=score_of[(final, h)],
                axis=mybir.AxisListType.X,
                op=mybir.AluOpType.max,
                negate=True,
            )
            exponential(final, h)
        normalise_and_store(final - 2)
        invert_sums(final - 1)
        normalise_and_store(final - 1)
        unit, rh = order[final][0], order[final][2]
        for h in range(2):
            nc.vector.reciprocal(out=inverse[:, h : h + 1], in_=row_sum_of[final][:, h : h + 1])
        for h in range(2):
            nc.vector.tensor_scalar_mul(
                out=weights_of[final][:, h, :], in0=weights_of[final][:, h, :], scalar1=inverse[:, h : h + 1]
            )
            nc.sync.dma_start(out=out[unit * 2 + h, rh * P : (rh + 1) * P, :], in_=weights_of[final][:, h, :])
